import numpy as np
import ml_dtypes


def mxq(x, axis, fmt="e4m3"):
    dtype, down = {"e4m3": (ml_dtypes.float8_e4m3fn, 7), "e5m2": (ml_dtypes.float8_e5m2, 14)}[fmt]
    v = np.moveaxis(np.asarray(x, np.float32).astype(ml_dtypes.bfloat16).astype(np.float64), axis, -1)
    blocks = v.reshape(v.shape[:-1] + (-1, 32))
    amax = np.abs(blocks).max(-1, keepdims=True)
    byte = np.maximum(np.where(amax > 0, np.frexp(amax)[1] - 1 + 127, 0) - down, 1)
    scale = np.exp2(byte - 127.0)
    codes = (blocks / scale).astype(np.float32).astype(dtype).astype(np.float64)
    return np.moveaxis((codes * scale).reshape(v.shape), -1, axis)


WIDE = False


def mx_kscale(k):
    if not WIDE:
        return np.ones(k)
    levels = np.array([10, -10, 5, -5, 0])
    if k % 512:
        return np.exp2(np.random.permutation(np.resize(levels, k // 32))).repeat(32)
    a = np.empty((k // 512, 16))
    for p in range(k // 512):
        a[p, :8] = np.random.permutation(np.resize(levels, 8))
        for g in range(8):
            far = levels[np.abs(levels - a[p, g]) >= 10]
            a[p, g + 8] = far[np.random.randint(len(far))]
    return np.exp2(a.ravel()).repeat(32)


BF16 = ml_dtypes.bfloat16


def bf(x):
    return np.asarray(x, np.float32).astype(BF16)


def f64(x):
    return np.asarray(x).astype(np.float64)


B, S, D, H, DH, DL, DR = 2, 2048, 1024, 2, 128, 512, 64
ROPE_BASE = 10000.0


def rope_cos_sin():
    inv_freq = 1.0 / ROPE_BASE ** (np.arange(0, DR, 2) / DR)
    freqs = np.arange(S)[:, None] * inv_freq[None, :]
    emb = np.concatenate([freqs, freqs], axis=-1)
    return np.cos(emb)[None, :, None, :], np.sin(emb)[None, :, None, :]


def rotate_half(u):
    u1, u2 = np.split(u, 2, axis=-1)
    return np.concatenate([-u2, u1], axis=-1)


def draw0():
    s, t = mx_kscale(D), mx_kscale(DL)
    return {"x": bf(np.random.standard_normal((B, S, D)) * s),
            "W_kv_down": bf(np.random.standard_normal((D, DL)) / np.sqrt(D) / s[:, None] * t),
            "W_kv_up": bf(np.random.standard_normal((DL, H * (DH + DR + DH))) / np.sqrt(DL) / t[:, None])}


def core(x, W_kv_down, W_kv_up):
    kv_latent = mxq(f64(x), 2, "e4m3") @ mxq(f64(W_kv_down), 0, "e4m3")
    kv_full = (mxq(kv_latent, 2, "e4m3") @ mxq(f64(W_kv_up), 0, "e4m3")).reshape(B, S, H, DH + DR + DH)
    k_content = kv_full[..., :DH]
    k_rope = kv_full[..., DH:DH + DR]
    v = kv_full[..., DH + DR:]
    cos, sin = rope_cos_sin()
    k_rope = k_rope * cos + rotate_half(k_rope) * sin
    k = np.concatenate([k_content, k_rope], axis=-1)
    return k, v


def e4m3fn_bytes(y):
    return np.clip(np.asarray(y, np.float64), -448.0, 448.0).astype(np.float32).astype(ml_dtypes.float8_e4m3fn).view(np.uint8)


def e4m3fn_values(b):
    return np.asarray(b, np.uint8).view(ml_dtypes.float8_e4m3fn).astype(np.float64)


def setup_inputs():
    d = draw0()
    x0 = np.asarray(d['x']).astype(np.float64)
    s = (np.max(np.abs(x0), axis=(0, 1), keepdims=True) / 448.0).astype(np.float32)
    out = {}
    for k, v in d.items():
        if k == 'x':
            out['x_bytes'] = e4m3fn_bytes(x0 / s.astype(np.float64))
            out['x_scale'] = s
        else:
            out[k] = v
    return out


def reference(x_bytes, x_scale, W_kv_down, W_kv_up):
    return core(e4m3fn_values(x_bytes) * x_scale.astype(np.float64), W_kv_down, W_kv_up)

@@ -1,0 +1,290 @@
+import math
+from contextlib import ExitStack
+
+import concourse.mybir as mybir
+from concourse.masks import make_identity
+
+F32 = mybir.dt.float32
+BF16 = mybir.dt.bfloat16
+U32 = mybir.dt.uint32
+I32 = mybir.dt.int32
+U8 = mybir.dt.uint8
+FP8 = mybir.dt.float8_e4m3fn
+FP8X4 = mybir.dt.float8_e4m3fn_x4
+ALU = mybir.AluOpType
+ACT = mybir.ActivationFunctionType
+
+B, S, D, H, DH, DL, DR = 2, 2048, 1024, 2, 128, 512, 64
+N_UP = H * (2 * DH + DR)
+FLOPS = 2 * B * S * D * DL + 2 * B * S * DL * N_UP
+
+P = 128
+GROUP = 4
+HALF = DR // 2
+N_GROUPS = B * S // (P * GROUP)
+POS_GROUPS = S // (P * GROUP)
+STEPS = N_GROUPS * 2
+TURN = 0.15915496
+C1 = 6.28125
+C2 = 2 * math.pi - C1
+
+
+def tile_multilatentattention_pa_t_kernel(tc, x_bytes, x_scale, w_down, w_up, out_k, out_v):
+    nc = tc.nc
+    x_view = x_bytes.rearrange("b (g q i) d -> (b g) q i d", q=P, i=GROUP)
+    k_view = out_k.rearrange("b (g q i) h f -> (b g) q i (h f)", q=P, i=GROUP)
+    v_view = out_v.rearrange("b (g q i) h f -> (b g) q i h f", q=P, i=GROUP)
+    wd_view = w_down.rearrange("(g p j) c -> g p j c", p=P, j=4)
+
+    with ExitStack() as ctx:
+        const = ctx.enter_context(tc.tile_pool(name="const", bufs=1))
+        xin = ctx.enter_context(tc.tile_pool(name="xin", bufs=N_GROUPS))
+        work = ctx.enter_context(tc.tile_pool(name="work", bufs=3))
+        outp = ctx.enter_context(tc.tile_pool(name="outp", bufs=3))
+        psum = ctx.enter_context(tc.psum_pool(name="psum", bufs=2))
+        ctx.enter_context(tc.manual_schedule())
+
+        wd_raw = const.tile([P, 2, 4, DL], BF16)
+        wu_raw = const.tile([P, 4, N_UP], BF16)
+        scale = const.tile([P, D], F32)
+        x_tiles = []
+        for g in range(N_GROUPS):
+            xb = xin.tile([P, GROUP, D], U8, name="xb")
+            x_tiles.append(xb)
+        nc.sync.dma_start(out=wd_raw[:, 0], in_=wd_view[0])
+        nc.sync.dma_start(out=wd_raw[:, 1], in_=wd_view[1])
+        nc.sync.dma_start(out=x_tiles[0][:, 0:2], in_=x_view[0][:, 0:2])
+        nc.sync.dma_start(out=scale[:], in_=x_scale.rearrange("a b d -> (a b d)").partition_broadcast(P))
+        nc.sync.dma_start(out=x_tiles[0][:, 2:4], in_=x_view[0][:, 2:4])
+        nc.sync.dma_start(out=wu_raw[:], in_=w_up.rearrange("(p j) n -> p j n", j=4))
+        for g in range(1, N_GROUPS):
+            nc.sync.dma_start(out=x_tiles[g][:], in_=x_view[g])
+
+        warm = const.tile([P, 1], F32)
+        nc.vector.memset(warm[:], 0.0)
+        nc.scalar.activation(out=warm[:], in_=warm[:], func=ACT.Sin)
+        pos = const.tile([P, POS_GROUPS, GROUP], F32)
+        nc.gpsimd.iota(pos[:], pattern=[[P * GROUP, POS_GROUPS], [1, GROUP]], base=0, channel_multiplier=GROUP, allow_small_or_imprecise_dtypes=True)
+        freq = const.tile([P, HALF], F32)
+        nc.gpsimd.memset(freq[:], 1.0)
+        for b in range(5):
+            f = freq[:].rearrange("p (x y z) -> p x y z", y=2, z=2 ** b)[:, :, 1, :]
+            nc.gpsimd.tensor_scalar(out=f, in0=f, scalar1=10000.0 ** (-(2 ** b) / HALF), scalar2=None, op0=ALU.mult)
+        ident = const.tile([P, P], F32)
+        make_identity(nc, ident[:])
+        shape = [P, POS_GROUPS * GROUP, HALF]
+        ang = const.tile(shape, F32)
+        turns = const.tile(shape, I32)
+        turns_f = const.tile(shape, F32)
+        red = const.tile(shape, F32)
+        red2 = const.tile(shape, F32)
+        mag = const.tile(shape, F32)
+        sin = const.tile(shape, F32)
+        cos = const.tile(shape, F32)
+        nc.vector.tensor_tensor(
+            out=ang[:],
+            in0=pos[:].rearrange("p a b -> p (a b)").unsqueeze(2).to_broadcast(shape),
+            in1=freq[:].unsqueeze(1).to_broadcast(shape),
+            op=ALU.mult,
+        )
+        nc.vector.tensor_scalar(out=turns[:], in0=ang[:], scalar1=TURN, scalar2=None, op0=ALU.mult)
+        nc.vector.tensor_copy(out=turns_f[:], in_=turns[:])
+        nc.vector.scalar_tensor_tensor(out=red[:], in0=turns_f[:], scalar=-C1, in1=ang[:], op0=ALU.mult, op1=ALU.add)
+        nc.vector.scalar_tensor_tensor(out=red2[:], in0=turns_f[:], scalar=-C2, in1=red[:], op0=ALU.mult, op1=ALU.add)
+
+        wd_grp = const.tile([P, 2, DL * 4], BF16, align_bytes=64)
+        wd_codes = const.tile([P, 2, DL], U32, align_bytes=64)
+        wd_scales = const.tile([P, 2, DL], U8, align_bytes=64)
+        wu_main_grp = const.tile([P, 2, H, DH, 4], BF16, align_bytes=64)
+        wu_rope_grp = const.tile([P, H, DR, 4], BF16, align_bytes=64)
+        wu_main_codes = const.tile([P, 4 * DH], U32, align_bytes=64)
+        wu_main_scales = const.tile([P, 4 * DH], U8, align_bytes=64)
+        wu_rope_codes = const.tile([P, H * DR], U32, align_bytes=64)
+        wu_rope_scales = const.tile([P, H * DR], U8, align_bytes=64)
+
+        def group_down(g, copy):
+            copy(
+                out=wd_grp[:, g].rearrange("p (t m j) -> p t m j", t=4, j=4),
+                in_=wd_raw[:, g].rearrange("p j (m t) -> p t m j", t=4),
+            )
+
+        def quant_down(g):
+            nc.vector.quantize_mx(out=wd_codes[:, g].bitcast(FP8X4), scales=wd_scales[:, g], in_=wd_grp[:, g])
+
+        group_down(0, nc.vector.tensor_copy)
+        group_down(1, nc.scalar.copy)
+        quant_down(0)
+        up = wu_raw[:].rearrange("p j (h f) -> p h f j", h=H)
+        nc.scalar.copy(out=wu_main_grp[:, 0], in_=up[:, :, 0:DH, :])
+        nc.scalar.copy(out=wu_main_grp[:, 1], in_=up[:, :, DH + DR:, :])
+        nc.scalar.copy(out=wu_rope_grp[:], in_=up[:, :, DH:DH + DR, :])
+        nc.scalar.activation(out=mag[:], in_=red2[:], func=ACT.Abs)
+        nc.scalar.activation(out=sin[:], in_=red2[:], func=ACT.Sin)
+        nc.scalar.activation(out=cos[:], in_=mag[:], func=ACT.Sin, scale=-1.0, bias=math.pi / 2)
+
+        def quant_up():
+            nc.vector.quantize_mx(out=wu_main_codes[:].bitcast(FP8X4), scales=wu_main_scales[:], in_=wu_main_grp[:].rearrange("p a h f j -> p (a h f j)"))
+            nc.vector.quantize_mx(out=wu_rope_codes[:].bitcast(FP8X4), scales=wu_rope_scales[:], in_=wu_rope_grp[:].rearrange("p h f j -> p (h f j)"))
+
+        xbf = {}
+        xt = {}
+        xg = {}
+        xc = {}
+        lat = {}
+        lg = {}
+        lc = {}
+        main = {}
+        rope = {}
+        kv = {}
+
+        def widen(s, i):
+            t = work.tile([P, D], BF16, name="xbf", bufs=6)
+            xbf[s, i] = t
+            nc.vector.tensor_tensor(out=t[:], in0=x_tiles[s // 2][:, 2 * (s % 2) + i].bitcast(FP8), in1=scale[:], op=ALU.mult)
+
+        def turn(s, i):
+            bank = psum.tile([P, 2, 2, P], F32, name="xt")
+            xt[s, i] = bank
+            words = xbf[s, i][:].bitcast(F32)
+            for g in range(2):
+                for u in range(2):
+                    nc.tensor.transpose(bank[:, g, u, :], words[:, 256 * g + u:256 * (g + 1):2], ident[:])
+
+        def empty_turn(s, i):
+            if i == 0:
+                xg[s] = work.tile([P, 2, 2, P * 4], BF16, name="xg", align_bytes=64)
+            nc.scalar.copy(
+                out=xg[s][:, i].bitcast(F32).rearrange("p g (r u) -> p g r u", u=2),
+                in_=xt[s, i][:].rearrange("p g u r -> p g r u"),
+            )
+
+        def quant_x(s):
+            codes = work.tile([P, 2, 2, P], U32, name="xcodes", align_bytes=64)
+            scales = work.tile([P, 2, 2, P], U8, name="xscales", align_bytes=64)
+            xc[s] = (codes, scales)
+            nc.vector.quantize_mx(
+                out=codes[:].rearrange("p i g r -> p (i g r)").bitcast(FP8X4),
+                scales=scales[:].rearrange("p i g r -> p (i g r)"),
+                in_=xg[s][:].rearrange("p i g c -> p (i g c)"),
+            )
+
+        def down(s, i):
+            bank = psum.tile([P, 4, P], F32, name="lat")
+            lat[s, i] = bank
+            codes, scales = xc[s]
+            for t in range(4):
+                for g in range(2):
+                    nc.tensor.matmul_mx(
+                        out=bank[:, t, :],
+                        lhsT=wd_codes[:, g, t * P:(t + 1) * P].bitcast(FP8X4),
+                        lhsT_scale=wd_scales[:, g, t * P:(t + 1) * P],
+                        rhs=codes[:, i, g].bitcast(FP8X4),
+                        rhs_scale=scales[:, i, g],
+                        start=(g == 0),
+                        stop=(g == 1),
+                    )
+
+        def empty_down(s, i):
+            if i == 0:
+                lg[s] = work.tile([P, 2, P, 4], BF16, name="lg", align_bytes=64, bufs=4)
+            nc.scalar.copy(out=lg[s][:, i], in_=lat[s, i][:].rearrange("p t r -> p r t"))
+
+        def quant_lat(s):
+            codes = work.tile([P, 2, P], U32, name="lcodes", align_bytes=64)
+            scales = work.tile([P, 2, P], U8, name="lscales", align_bytes=64)
+            lc[s] = (codes, scales)
+            nc.vector.quantize_mx(
+                out=codes[:].rearrange("p i r -> p (i r)").bitcast(FP8X4),
+                scales=scales[:].rearrange("p i r -> p (i r)"),
+                in_=lg[s][:].rearrange("p i r t -> p (i r t)"),
+            )
+
+        def expand(s, i):
+            if s % 2 == 0 and i == 0:
+                rope[s // 2] = psum.tile([P, GROUP, H, 2, HALF], F32, name="rope")
+            bank = psum.tile([P, 4, DH], F32, name="main")
+            main[s, i] = bank
+            codes, scales = lc[s]
+            nc.tensor.matmul_mx(
+                out=bank[:].rearrange("p a f -> p (a f)"),
+                lhsT=codes[:, i].bitcast(FP8X4), lhsT_scale=scales[:, i],
+                rhs=wu_main_codes[:].bitcast(FP8X4), rhs_scale=wu_main_scales[:],
+                start=True, stop=True,
+            )
+            nc.tensor.matmul_mx(
+                out=rope[s // 2][:, 2 * (s % 2) + i].rearrange("p h a f -> p (h a f)"),
+                lhsT=codes[:, i].bitcast(FP8X4), lhsT_scale=scales[:, i],
+                rhs=wu_rope_codes[:].bitcast(FP8X4), rhs_scale=wu_rope_scales[:],
+                start=True, stop=True,
+            )
+
+        def empty_main(s, i):
+            if s % 2 == 0 and i == 0:
+                kv[s // 2] = outp.tile([P, GROUP, 4, DH + DR], F32, name="kv")
+            nc.scalar.copy(out=kv[s // 2][:, 2 * (s % 2) + i, :, 0:DH], in_=main[s, i][:])
+
+        rot = {}
+
+        def rope_mul(g):
+            a = work.tile([P, GROUP, H, 2, HALF], F32, name="rot_a", bufs=2)
+            b = work.tile([P, GROUP, H, 2, HALF], F32, name="rot_b", bufs=2)
+            rot[g] = (a, b)
+            first = (g % POS_GROUPS) * GROUP
+            full = [P, GROUP, 2 * H, HALF]
+            for dst, table in ((a, cos), (b, sin)):
+                nc.vector.tensor_tensor(
+                    out=dst[:].rearrange("p i h a f -> p i (h a) f"),
+                    in0=rope[g][:].rearrange("p i h a f -> p i (h a) f"),
+                    in1=table[:, first:first + GROUP].unsqueeze(2).to_broadcast(full),
+                    op=ALU.mult,
+                )
+
+        def rope_add(g):
+            a, b = rot[g]
+            o = kv[g]
+            nc.vector.tensor_tensor(out=o[:, :, 0:H, DH:DH + HALF], in0=a[:, :, :, 0], in1=b[:, :, :, 1], op=ALU.subtract)
+            nc.vector.tensor_tensor(out=o[:, :, 0:H, DH + HALF:], in0=a[:, :, :, 1], in1=b[:, :, :, 0], op=ALU.add)
+
+        def store_v(g):
+            for h in range(H):
+                nc.sync.dma_start(out=v_view[g][:, :, h], in_=kv[g][:, :, 2 + h, 0:DH])
+
+        def store_k(g):
+            nc.sync.dma_start(out=k_view[g], in_=kv[g][:, :, 0:2, :].rearrange("p i h f -> p i (h f)"))
+
+        for it in range(STEPS + 5):
+            now, mid, old = it, it - 1, it - 3
+            if 0 <= old < STEPS:
+                quant_lat(old)
+                for i in range(2):
+                    expand(old, i)
+            if now < STEPS:
+                widen(now, 0)
+                turn(now, 0)
+            if it == 0:
+                quant_down(1)
+            if 0 <= mid < STEPS:
+                quant_x(mid)
+                for i in range(2):
+                    down(mid, i)
+            if it == 2:
+                quant_up()
+            if 0 <= old < STEPS:
+                for i in range(2):
+                    empty_main(old, i)
+                if old % 2:
+                    store_v(old // 2)
+            if now < STEPS:
+                empty_turn(now, 0)
+            if 0 <= mid < STEPS:
+                for i in range(2):
+                    empty_down(mid, i)
+            if now < STEPS:
+                widen(now, 1)
+                turn(now, 1)
+                empty_turn(now, 1)
+            if 0 <= old < STEPS and old % 2:
+                rope_mul(old // 2)
+            if it >= 5 and it % 2 == 1 and (it - 5) // 2 < N_GROUPS:
+                rope_add((it - 5) // 2)
+                store_k((it - 5) // 2)

@@ -51,13 +51,15 @@ def tile_multilatentattention_pa_t_kernel(tc, x_bytes, x_scale, w_down, w_up, ou
         for g in range(N_GROUPS):
             xb = xin.tile([P, GROUP, D], U8, name="xb")
             x_tiles.append(xb)
+        scale_cols = const.tile([P, 2, 4], F32)
+        nc.sync.dma_start(out=scale_cols[:], in_=x_scale.rearrange("a b (g p t) -> p (a b g) t", p=P, t=4))
         nc.sync.dma_start(out=wd_raw[:, 0], in_=wd_view[0])
-        nc.sync.dma_start(out=wd_raw[:, 1], in_=wd_view[1])
         nc.sync.dma_start(out=x_tiles[0][:, 0:2], in_=x_view[0][:, 0:2])
-        nc.sync.dma_start(out=scale[:], in_=x_scale.rearrange("a b d -> (a b d)").partition_broadcast(P))
+        nc.sync.dma_start(out=wd_raw[:, 1], in_=wd_view[1])
         nc.sync.dma_start(out=x_tiles[0][:, 2:4], in_=x_view[0][:, 2:4])
+        nc.sync.dma_start(out=x_tiles[1][:], in_=x_view[1])
         nc.sync.dma_start(out=wu_raw[:], in_=w_up.rearrange("(p j) n -> p j n", j=4))
-        for g in range(1, N_GROUPS):
+        for g in range(2, N_GROUPS):
             nc.sync.dma_start(out=x_tiles[g][:], in_=x_view[g])
 
         warm = const.tile([P, 1], F32)
@@ -65,12 +67,12 @@ def tile_multilatentattention_pa_t_kernel(tc, x_bytes, x_scale, w_down, w_up, ou
         nc.scalar.activation(out=warm[:], in_=warm[:], func=ACT.Sin)
         pos = const.tile([P, POS_GROUPS, GROUP], F32)
         nc.gpsimd.iota(pos[:], pattern=[[P * GROUP, POS_GROUPS], [1, GROUP]], base=0, channel_multiplier=GROUP, allow_small_or_imprecise_dtypes=True)
+        ident = const.tile([P, P], F32)
         freq = const.tile([P, HALF], F32)
         nc.gpsimd.memset(freq[:], 1.0)
         for b in range(5):
             f = freq[:].rearrange("p (x y z) -> p x y z", y=2, z=2 ** b)[:, :, 1, :]
             nc.gpsimd.tensor_scalar(out=f, in0=f, scalar1=10000.0 ** (-(2 ** b) / HALF), scalar2=None, op0=ALU.mult)
-        ident = const.tile([P, P], F32)
         make_identity(nc, ident[:])
         shape = [P, POS_GROUPS * GROUP, HALF]
         ang = const.tile(shape, F32)
@@ -79,7 +81,7 @@ def tile_multilatentattention_pa_t_kernel(tc, x_bytes, x_scale, w_down, w_up, ou
         red = const.tile(shape, F32)
         red2 = const.tile(shape, F32)
         mag = const.tile(shape, F32)
-        sin = const.tile(shape, F32)
+        sin = const.tile([P, POS_GROUPS * GROUP, 2, HALF], F32)
         cos = const.tile(shape, F32)
         nc.vector.tensor_tensor(
             out=ang[:],
@@ -111,16 +113,27 @@ def tile_multilatentattention_pa_t_kernel(tc, x_bytes, x_scale, w_down, w_up, ou
         def quant_down(g):
             nc.vector.quantize_mx(out=wd_codes[:, g].bitcast(FP8X4), scales=wd_scales[:, g], in_=wd_grp[:, g])
 
+        for g in range(2):
+            bank = psum.tile([P, 4, P], F32, name="xt")
+            for t in range(4):
+                nc.tensor.transpose(bank[:, t, :], scale_cols[:, g, t:t + 1].to_broadcast([P, P]), ident[:])
+            nc.scalar.copy(out=scale[:, g * 512:(g + 1) * 512].rearrange("p (n t) -> p n t", t=4), in_=bank[:].rearrange("p t n -> p n t"))
         group_down(0, nc.vector.tensor_copy)
-        group_down(1, nc.scalar.copy)
         quant_down(0)
+        group_down(1, nc.scalar.copy)
         up = wu_raw[:].rearrange("p j (h f) -> p h f j", h=H)
-        nc.scalar.copy(out=wu_main_grp[:, 0], in_=up[:, :, 0:DH, :])
-        nc.scalar.copy(out=wu_main_grp[:, 1], in_=up[:, :, DH + DR:, :])
-        nc.scalar.copy(out=wu_rope_grp[:], in_=up[:, :, DH:DH + DR, :])
-        nc.scalar.activation(out=mag[:], in_=red2[:], func=ACT.Abs)
-        nc.scalar.activation(out=sin[:], in_=red2[:], func=ACT.Sin)
-        nc.scalar.activation(out=cos[:], in_=mag[:], func=ACT.Sin, scale=-1.0, bias=math.pi / 2)
+        for dst, src in (
+            (wu_main_grp[:, 0], up[:, :, 0:DH, :]),
+            (wu_main_grp[:, 1], up[:, :, DH + DR:, :]),
+            (wu_rope_grp[:], up[:, :, DH:DH + DR, :]),
+        ):
+            nc.gpsimd.tensor_scalar(out=dst, in0=src, scalar1=1.0, scalar2=0.0, op0=ALU.mult, op1=ALU.add)
+
+        def tables():
+            nc.scalar.activation(out=mag[:], in_=red2[:], func=ACT.Abs)
+            nc.scalar.activation(out=cos[:], in_=mag[:], func=ACT.Sin, scale=-1.0, bias=math.pi / 2)
+            nc.scalar.activation(out=sin[:, :, 0], in_=red2[:], func=ACT.Sin)
+            nc.scalar.activation(out=sin[:, :, 1], in_=red2[:], func=ACT.Sin, scale=-1.0)
 
         def quant_up():
             nc.vector.quantize_mx(out=wu_main_codes[:].bitcast(FP8X4), scales=wu_main_scales[:], in_=wu_main_grp[:].rearrange("p a h f j -> p (a h f j)"))
@@ -225,66 +238,79 @@ def tile_multilatentattention_pa_t_kernel(tc, x_bytes, x_scale, w_down, w_up, ou
 
         rot = {}
 
-        def rope_mul(g):
-            a = work.tile([P, GROUP, H, 2, HALF], F32, name="rot_a", bufs=2)
-            b = work.tile([P, GROUP, H, 2, HALF], F32, name="rot_b", bufs=2)
-            rot[g] = (a, b)
-            first = (g % POS_GROUPS) * GROUP
-            full = [P, GROUP, 2 * H, HALF]
-            for dst, table in ((a, cos), (b, sin)):
-                nc.vector.tensor_tensor(
-                    out=dst[:].rearrange("p i h a f -> p i (h a) f"),
-                    in0=rope[g][:].rearrange("p i h a f -> p i (h a) f"),
-                    in1=table[:, first:first + GROUP].unsqueeze(2).to_broadcast(full),
-                    op=ALU.mult,
-                )
+        def rope_mul(g, lo, n):
+            a = work.tile([P, n, H, 2, HALF], F32, name="rot_a", bufs=3)
+            b = work.tile([P, n, H, 2, HALF], F32, name="rot_b", bufs=3)
+            rot[g, lo] = (a, b)
+            first = (g % POS_GROUPS) * GROUP + lo
+            bank = rope[g][:, lo:lo + n]
+            nc.vector.tensor_tensor(
+                out=a[:].rearrange("p i h a f -> p i (h a) f"),
+                in0=bank.rearrange("p i h a f -> p i (h a) f"),
+                in1=cos[:, first:first + n].unsqueeze(2).to_broadcast([P, n, 2 * H, HALF]),
+                op=ALU.mult,
+            )
+            nc.vector.tensor_tensor(
+                out=b[:].rearrange("p i h a f -> p i h (a f)"),
+                in0=bank.rearrange("p i h a f -> p i h (a f)"),
+                in1=sin[:, first:first + n].rearrange("p i a f -> p i (a f)").unsqueeze(2).to_broadcast([P, n, H, DR]),
+                op=ALU.mult,
+            )
 
-        def rope_add(g):
-            a, b = rot[g]
-            o = kv[g]
-            nc.vector.tensor_tensor(out=o[:, :, 0:H, DH:DH + HALF], in0=a[:, :, :, 0], in1=b[:, :, :, 1], op=ALU.subtract)
-            nc.vector.tensor_tensor(out=o[:, :, 0:H, DH + HALF:], in0=a[:, :, :, 1], in1=b[:, :, :, 0], op=ALU.add)
+        def rope_add(g, lo, n):
+            a, b = rot[g, lo]
+            nc.vector.tensor_tensor(
+                out=kv[g][:, lo:lo + n, 0:H, DH:].rearrange("p i h (a f) -> p i h a f", a=2),
+                in0=a[:], in1=b[:, :, :, ::-1, :], op=ALU.add,
+            )
 
         def store_v(g):
             for h in range(H):
                 nc.sync.dma_start(out=v_view[g][:, :, h], in_=kv[g][:, :, 2 + h, 0:DH])
 
-        def store_k(g):
-            nc.sync.dma_start(out=k_view[g], in_=kv[g][:, :, 0:2, :].rearrange("p i h f -> p i (h f)"))
+        def store_k(g, lo, n):
+            nc.sync.dma_start(out=k_view[g][:, lo:lo + n], in_=kv[g][:, lo:lo + n, 0:2, :].rearrange("p i h f -> p i (h f)"))
 
-        for it in range(STEPS + 5):
-            now, mid, old = it, it - 1, it - 3
-            if 0 <= old < STEPS:
-                quant_lat(old)
-                for i in range(2):
-                    expand(old, i)
+        for it in range(STEPS + 3):
+            now, mid, old, mul, end = it, it - 1, it - 3, it - 4, it - 5
             if now < STEPS:
                 widen(now, 0)
                 turn(now, 0)
-            if it == 0:
-                quant_down(1)
-            if 0 <= mid < STEPS:
-                quant_x(mid)
-                for i in range(2):
-                    down(mid, i)
-            if it == 2:
-                quant_up()
-            if 0 <= old < STEPS:
-                for i in range(2):
-                    empty_main(old, i)
-                if old % 2:
-                    store_v(old // 2)
-            if now < STEPS:
-                empty_turn(now, 0)
-            if 0 <= mid < STEPS:
-                for i in range(2):
-                    empty_down(mid, i)
-            if now < STEPS:
                 widen(now, 1)
                 turn(now, 1)
+            if it == 0:
+                quant_down(1)
+            if 0 <= old < STEPS:
+                quant_lat(old)
+                expand(old, 0)
+                expand(old, 1)
+            if 0 <= end < STEPS and end % 2:
+                rope_add(end // 2, 0, GROUP)
+                store_k(end // 2, 0, GROUP)
+            if 0 <= mid < STEPS:
+                quant_x(mid)
+                down(mid, 0)
+                down(mid, 1)
+            if it == 1:
+                quant_up()
+            if 0 <= mul < STEPS and mul % 2:
+                rope_mul(mul // 2, 0, GROUP)
+            if now < STEPS:
+                empty_turn(now, 0)
                 empty_turn(now, 1)
-            if 0 <= old < STEPS and old % 2:
-                rope_mul(old // 2)
-            if it >= 5 and it % 2 == 1 and (it - 5) // 2 < N_GROUPS:
-                rope_add((it - 5) // 2)
-                store_k((it - 5) // 2)
+            if it == 1:
+                tables()
+            if 0 <= old < STEPS:
+                empty_main(old, 0)
+                empty_main(old, 1)
+                if old % 2:
+                    store_v(old // 2)
+            if 0 <= mid < STEPS:
+                empty_down(mid, 0)
+                empty_down(mid, 1)
+        last = N_GROUPS - 1
+        for lo in (0, 2):
+            rope_mul(last, lo, 2)
+        for lo in (0, 2):
+            rope_add(last, lo, 2)
+            store_k(last, lo, 2)

@@ -46,19 +46,18 @@ def tile_multilatentattention_pa_t_kernel(tc, x_bytes, x_scale, w_down, w_up, ou
 
         wd_raw = const.tile([P, 2, 4, DL], BF16)
         wu_raw = const.tile([P, 4, N_UP], BF16)
-        scale = const.tile([P, D], F32)
         x_tiles = []
         for g in range(N_GROUPS):
             xb = xin.tile([P, GROUP, D], U8, name="xb")
             x_tiles.append(xb)
         scale_cols = const.tile([P, 2, 4], F32)
         nc.sync.dma_start(out=scale_cols[:], in_=x_scale.rearrange("a b (g p t) -> p (a b g) t", p=P, t=4))
-        nc.sync.dma_start(out=wd_raw[:, 0], in_=wd_view[0])
         nc.sync.dma_start(out=x_tiles[0][:, 0:2], in_=x_view[0][:, 0:2])
+        nc.sync.dma_start(out=wd_raw[:, 0], in_=wd_view[0])
         nc.sync.dma_start(out=wd_raw[:, 1], in_=wd_view[1])
         nc.sync.dma_start(out=x_tiles[0][:, 2:4], in_=x_view[0][:, 2:4])
-        nc.sync.dma_start(out=x_tiles[1][:], in_=x_view[1])
         nc.sync.dma_start(out=wu_raw[:], in_=w_up.rearrange("(p j) n -> p j n", j=4))
+        nc.sync.dma_start(out=x_tiles[1][:], in_=x_view[1])
         for g in range(2, N_GROUPS):
             nc.sync.dma_start(out=x_tiles[g][:], in_=x_view[g])
 
@@ -68,12 +67,12 @@ def tile_multilatentattention_pa_t_kernel(tc, x_bytes, x_scale, w_down, w_up, ou
         pos = const.tile([P, POS_GROUPS, GROUP], F32)
         nc.gpsimd.iota(pos[:], pattern=[[P * GROUP, POS_GROUPS], [1, GROUP]], base=0, channel_multiplier=GROUP, allow_small_or_imprecise_dtypes=True)
         ident = const.tile([P, P], F32)
+        make_identity(nc, ident[:])
         freq = const.tile([P, HALF], F32)
-        nc.gpsimd.memset(freq[:], 1.0)
+        nc.vector.memset(freq[:], 1.0)
         for b in range(5):
             f = freq[:].rearrange("p (x y z) -> p x y z", y=2, z=2 ** b)[:, :, 1, :]
-            nc.gpsimd.tensor_scalar(out=f, in0=f, scalar1=10000.0 ** (-(2 ** b) / HALF), scalar2=None, op0=ALU.mult)
-        make_identity(nc, ident[:])
+            nc.vector.tensor_scalar(out=f, in0=f, scalar1=10000.0 ** (-(2 ** b) / HALF), scalar2=None, op0=ALU.mult)
         shape = [P, POS_GROUPS * GROUP, HALF]
         ang = const.tile(shape, F32)
         turns = const.tile(shape, I32)
@@ -113,21 +112,17 @@ def tile_multilatentattention_pa_t_kernel(tc, x_bytes, x_scale, w_down, w_up, ou
         def quant_down(g):
             nc.vector.quantize_mx(out=wd_codes[:, g].bitcast(FP8X4), scales=wd_scales[:, g], in_=wd_grp[:, g])
 
-        for g in range(2):
-            bank = psum.tile([P, 4, P], F32, name="xt")
-            for t in range(4):
-                nc.tensor.transpose(bank[:, t, :], scale_cols[:, g, t:t + 1].to_broadcast([P, P]), ident[:])
-            nc.scalar.copy(out=scale[:, g * 512:(g + 1) * 512].rearrange("p (n t) -> p n t", t=4), in_=bank[:].rearrange("p t n -> p n t"))
         group_down(0, nc.vector.tensor_copy)
         quant_down(0)
-        group_down(1, nc.scalar.copy)
         up = wu_raw[:].rearrange("p j (h f) -> p h f j", h=H)
-        for dst, src in (
-            (wu_main_grp[:, 0], up[:, :, 0:DH, :]),
-            (wu_main_grp[:, 1], up[:, :, DH + DR:, :]),
-            (wu_rope_grp[:], up[:, :, DH:DH + DR, :]),
-        ):
-            nc.gpsimd.tensor_scalar(out=dst, in0=src, scalar1=1.0, scalar2=0.0, op0=ALU.mult, op1=ALU.add)
+
+        def group_up():
+            for dst, src in (
+                (wu_main_grp[:, 0], up[:, :, 0:DH, :]),
+                (wu_main_grp[:, 1], up[:, :, DH + DR:, :]),
+                (wu_rope_grp[:], up[:, :, DH:DH + DR, :]),
+            ):
+                nc.scalar.copy(out=dst, in_=src)
 
         def tables():
             nc.scalar.activation(out=mag[:], in_=red2[:], func=ACT.Abs)
@@ -151,9 +146,9 @@ def tile_multilatentattention_pa_t_kernel(tc, x_bytes, x_scale, w_down, w_up, ou
         kv = {}
 
         def widen(s, i):
-            t = work.tile([P, D], BF16, name="xbf", bufs=6)
+            t = work.tile([P, D], BF16, name="xbf", bufs=8)
             xbf[s, i] = t
-            nc.vector.tensor_tensor(out=t[:], in0=x_tiles[s // 2][:, 2 * (s % 2) + i].bitcast(FP8), in1=scale[:], op=ALU.mult)
+            nc.scalar.copy(out=t[:], in_=x_tiles[s // 2][:, 2 * (s % 2) + i].bitcast(FP8))
 
         def turn(s, i):
             bank = psum.tile([P, 2, 2, P], F32, name="xt")
@@ -161,14 +156,16 @@ def tile_multilatentattention_pa_t_kernel(tc, x_bytes, x_scale, w_down, w_up, ou
             words = xbf[s, i][:].bitcast(F32)
             for g in range(2):
                 for u in range(2):
-                    nc.tensor.transpose(bank[:, g, u, :], words[:, 256 * g + u:256 * (g + 1):2], ident[:])
+                    nc.tensor.transpose(bank[:, u, g, :], words[:, 256 * g + u:256 * (g + 1):2], ident[:])
 
         def empty_turn(s, i):
             if i == 0:
                 xg[s] = work.tile([P, 2, 2, P * 4], BF16, name="xg", align_bytes=64)
-            nc.scalar.copy(
-                out=xg[s][:, i].bitcast(F32).rearrange("p g (r u) -> p g r u", u=2),
-                in_=xt[s, i][:].rearrange("p g u r -> p g r u"),
+            nc.vector.tensor_tensor(
+                out=xg[s][:, i].rearrange("p g (r u e) -> p g r u e", u=2, e=2),
+                in0=xt[s, i][:].bitcast(BF16).rearrange("p u g (r e) -> p g r u e", e=2),
+                in1=scale_cols[:].rearrange("p g (u e) -> p g u e", u=2).unsqueeze(2).to_broadcast([P, 2, P, 2, 2]),
+                op=ALU.mult,
             )
 
         def quant_x(s):
@@ -264,6 +261,14 @@ def tile_multilatentattention_pa_t_kernel(tc, x_bytes, x_scale, w_down, w_up, ou
                 in0=a[:], in1=b[:, :, :, ::-1, :], op=ALU.add,
             )
 
+        def rope_add_beside(g):
+            a, b = rot[g, 0]
+            for half in range(2):
+                nc.gpsimd.tensor_tensor(
+                    out=kv[g][:, :, 0:H, DH + half * HALF:DH + (half + 1) * HALF],
+                    in0=a[:, :, :, half], in1=b[:, :, :, 1 - half], op=ALU.add,
+                )
+
         def store_v(g):
             for h in range(H):
                 nc.sync.dma_start(out=v_view[g][:, :, h], in_=kv[g][:, :, 2 + h, 0:DH])
@@ -271,46 +276,54 @@ def tile_multilatentattention_pa_t_kernel(tc, x_bytes, x_scale, w_down, w_up, ou
         def store_k(g, lo, n):
             nc.sync.dma_start(out=k_view[g][:, lo:lo + n], in_=kv[g][:, lo:lo + n, 0:2, :].rearrange("p i h f -> p i (h f)"))
 
-        for it in range(STEPS + 3):
-            now, mid, old, mul, end = it, it - 1, it - 3, it - 4, it - 5
-            if now < STEPS:
-                widen(now, 0)
-                turn(now, 0)
-                widen(now, 1)
-                turn(now, 1)
-            if it == 0:
+        for it in range(-2, STEPS + 4):
+            wide, now, mid, lat_q, old, mul = it + 2, it, it - 1, it - 3, it - 4, it - 5
+            if it == 1:
                 quant_down(1)
+            if 0 <= now < STEPS:
+                turn(now, 0)
+            if 0 <= lat_q < STEPS:
+                quant_lat(lat_q)
             if 0 <= old < STEPS:
-                quant_lat(old)
                 expand(old, 0)
                 expand(old, 1)
-            if 0 <= end < STEPS and end % 2:
-                rope_add(end // 2, 0, GROUP)
-                store_k(end // 2, 0, GROUP)
+            if 0 <= now < STEPS:
+                turn(now, 1)
             if 0 <= mid < STEPS:
                 quant_x(mid)
                 down(mid, 0)
                 down(mid, 1)
-            if it == 1:
-                quant_up()
-            if 0 <= mul < STEPS and mul % 2:
+            if 0 <= mul < STEPS - 1 and mul % 2:
                 rope_mul(mul // 2, 0, GROUP)
-            if now < STEPS:
+                rope_add_beside(mul // 2)
+            if 0 <= now < STEPS:
                 empty_turn(now, 0)
                 empty_turn(now, 1)
-            if it == 1:
-                tables()
+            if it == 2:
+                quant_up()
             if 0 <= old < STEPS:
                 empty_main(old, 0)
                 empty_main(old, 1)
                 if old % 2:
                     store_v(old // 2)
+            if wide < STEPS:
+                widen(wide, 0)
             if 0 <= mid < STEPS:
                 empty_down(mid, 0)
                 empty_down(mid, 1)
+            if wide < STEPS:
+                widen(wide, 1)
+            if it == -2:
+                group_down(1, nc.scalar.copy)
+            if it == 0:
+                group_up()
+            if it == 3:
+                tables()
+            if 0 <= mul < STEPS - 1 and mul % 2:
+                store_k(mul // 2, 0, GROUP)
         last = N_GROUPS - 1
-        for lo in (0, 2):
-            rope_mul(last, lo, 2)
+        rope_mul(last, 0, 2)
+        rope_mul(last, 2, 2)
         for lo in (0, 2):
             rope_add(last, lo, 2)
             store_k(last, lo, 2)

import math
from contextlib import ExitStack

import concourse.mybir as mybir
from concourse.masks import make_identity

F32 = mybir.dt.float32
BF16 = mybir.dt.bfloat16
U32 = mybir.dt.uint32
I32 = mybir.dt.int32
U8 = mybir.dt.uint8
FP8 = mybir.dt.float8_e4m3fn
FP8X4 = mybir.dt.float8_e4m3fn_x4
ALU = mybir.AluOpType
ACT = mybir.ActivationFunctionType

B, S, D, H, DH, DL, DR = 2, 2048, 1024, 2, 128, 512, 64
N_UP = H * (2 * DH + DR)
FLOPS = 2 * B * S * D * DL + 2 * B * S * DL * N_UP

P = 128
GROUP = 4
HALF = DR // 2
N_GROUPS = B * S // (P * GROUP)
POS_GROUPS = S // (P * GROUP)
STEPS = N_GROUPS * 2
TURN = 0.15915496
C1 = 6.28125
C2 = 2 * math.pi - C1


def tile_multilatentattention_pa_t_kernel(tc, x_bytes, x_scale, w_down, w_up, out_k, out_v):
    nc = tc.nc
    x_view = x_bytes.rearrange("b (g q i) d -> (b g) q i d", q=P, i=GROUP)
    k_view = out_k.rearrange("b (g q i) h f -> (b g) q i (h f)", q=P, i=GROUP)
    v_view = out_v.rearrange("b (g q i) h f -> (b g) q i h f", q=P, i=GROUP)
    wd_view = w_down.rearrange("(g p j) c -> g p j c", p=P, j=4)

    with ExitStack() as ctx:
        const = ctx.enter_context(tc.tile_pool(name="const", bufs=1))
        xin = ctx.enter_context(tc.tile_pool(name="xin", bufs=N_GROUPS))
        work = ctx.enter_context(tc.tile_pool(name="work", bufs=3))
        outp = ctx.enter_context(tc.tile_pool(name="outp", bufs=3))
        psum = ctx.enter_context(tc.psum_pool(name="psum", bufs=2))
        ctx.enter_context(tc.manual_schedule())

        wd_raw = const.tile([P, 2, 4, DL], BF16)
        wu_raw = const.tile([P, 4, N_UP], BF16)
        x_tiles = []
        for g in range(N_GROUPS):
            xb = xin.tile([P, GROUP, D], U8, name="xb")
            x_tiles.append(xb)
        scale_cols = const.tile([P, 2, 4], F32)
        nc.sync.dma_start(out=scale_cols[:], in_=x_scale.rearrange("a b (g p t) -> p (a b g) t", p=P, t=4))
        nc.sync.dma_start(out=x_tiles[0][:, 0:2], in_=x_view[0][:, 0:2])
        nc.sync.dma_start(out=wd_raw[:, 0], in_=wd_view[0])
        nc.sync.dma_start(out=wd_raw[:, 1], in_=wd_view[1])
        nc.sync.dma_start(out=x_tiles[0][:, 2:4], in_=x_view[0][:, 2:4])
        nc.sync.dma_start(out=wu_raw[:], in_=w_up.rearrange("(p j) n -> p j n", j=4))
        nc.sync.dma_start(out=x_tiles[1][:], in_=x_view[1])
        for g in range(2, N_GROUPS):
            nc.sync.dma_start(out=x_tiles[g][:], in_=x_view[g])

        warm = const.tile([P, 1], F32)
        nc.vector.memset(warm[:], 0.0)
        nc.scalar.activation(out=warm[:], in_=warm[:], func=ACT.Sin)
        pos = const.tile([P, POS_GROUPS, GROUP], F32)
        nc.gpsimd.iota(pos[:], pattern=[[P * GROUP, POS_GROUPS], [1, GROUP]], base=0, channel_multiplier=GROUP, allow_small_or_imprecise_dtypes=True)
        ident = const.tile([P, P], F32)
        make_identity(nc, ident[:])
        freq = const.tile([P, HALF], F32)
        nc.vector.memset(freq[:], 1.0)
        for b in range(5):
            f = freq[:].rearrange("p (x y z) -> p x y z", y=2, z=2 ** b)[:, :, 1, :]
            nc.vector.tensor_scalar(out=f, in0=f, scalar1=10000.0 ** (-(2 ** b) / HALF), scalar2=None, op0=ALU.mult)
        shape = [P, POS_GROUPS * GROUP, HALF]
        ang = const.tile(shape, F32)
        turns = const.tile(shape, I32)
        turns_f = const.tile(shape, F32)
        red = const.tile(shape, F32)
        red2 = const.tile(shape, F32)
        mag = const.tile(shape, F32)
        sin = const.tile([P, POS_GROUPS * GROUP, 2, HALF], F32)
        cos = const.tile(shape, F32)
        nc.vector.tensor_tensor(
            out=ang[:],
            in0=pos[:].rearrange("p a b -> p (a b)").unsqueeze(2).to_broadcast(shape),
            in1=freq[:].unsqueeze(1).to_broadcast(shape),
            op=ALU.mult,
        )
        nc.vector.tensor_scalar(out=turns[:], in0=ang[:], scalar1=TURN, scalar2=None, op0=ALU.mult)
        nc.vector.tensor_copy(out=turns_f[:], in_=turns[:])
        nc.vector.scalar_tensor_tensor(out=red[:], in0=turns_f[:], scalar=-C1, in1=ang[:], op0=ALU.mult, op1=ALU.add)
        nc.vector.scalar_tensor_tensor(out=red2[:], in0=turns_f[:], scalar=-C2, in1=red[:], op0=ALU.mult, op1=ALU.add)

        wd_grp = const.tile([P, 2, DL * 4], BF16, align_bytes=64)
        wd_codes = const.tile([P, 2, DL], U32, align_bytes=64)
        wd_scales = const.tile([P, 2, DL], U8, align_bytes=64)
        wu_main_grp = const.tile([P, 2, H, DH, 4], BF16, align_bytes=64)
        wu_rope_grp = const.tile([P, H, DR, 4], BF16, align_bytes=64)
        wu_main_codes = const.tile([P, 4 * DH], U32, align_bytes=64)
        wu_main_scales = const.tile([P, 4 * DH], U8, align_bytes=64)
        wu_rope_codes = const.tile([P, H * DR], U32, align_bytes=64)
        wu_rope_scales = const.tile([P, H * DR], U8, align_bytes=64)

        def group_down(g, copy):
            copy(
                out=wd_grp[:, g].rearrange("p (t m j) -> p t m j", t=4, j=4),
                in_=wd_raw[:, g].rearrange("p j (m t) -> p t m j", t=4),
            )

        def quant_down(g):
            nc.vector.quantize_mx(out=wd_codes[:, g].bitcast(FP8X4), scales=wd_scales[:, g], in_=wd_grp[:, g])

        group_down(0, nc.vector.tensor_copy)
        quant_down(0)
        up = wu_raw[:].rearrange("p j (h f) -> p h f j", h=H)

        def group_up():
            for dst, src in (
                (wu_main_grp[:, 0], up[:, :, 0:DH, :]),
                (wu_main_grp[:, 1], up[:, :, DH + DR:, :]),
                (wu_rope_grp[:], up[:, :, DH:DH + DR, :]),
            ):
                nc.scalar.copy(out=dst, in_=src)

        def tables():
            nc.scalar.activation(out=mag[:], in_=red2[:], func=ACT.Abs)
            nc.scalar.activation(out=cos[:], in_=mag[:], func=ACT.Sin, scale=-1.0, bias=math.pi / 2)
            nc.scalar.activation(out=sin[:, :, 0], in_=red2[:], func=ACT.Sin)
            nc.scalar.activation(out=sin[:, :, 1], in_=red2[:], func=ACT.Sin, scale=-1.0)

        def quant_up():
            nc.vector.quantize_mx(out=wu_main_codes[:].bitcast(FP8X4), scales=wu_main_scales[:], in_=wu_main_grp[:].rearrange("p a h f j -> p (a h f j)"))
            nc.vector.quantize_mx(out=wu_rope_codes[:].bitcast(FP8X4), scales=wu_rope_scales[:], in_=wu_rope_grp[:].rearrange("p h f j -> p (h f j)"))

        xbf = {}
        xt = {}
        xg = {}
        xc = {}
        lat = {}
        lg = {}
        lc = {}
        main = {}
        rope = {}
        kv = {}

        def widen(s, i):
            t = work.tile([P, D], BF16, name="xbf", bufs=8)
            xbf[s, i] = t
            nc.scalar.copy(out=t[:], in_=x_tiles[s // 2][:, 2 * (s % 2) + i].bitcast(FP8))

        def turn(s, i):
            bank = psum.tile([P, 2, 2, P], F32, name="xt")
            xt[s, i] = bank
            words = xbf[s, i][:].bitcast(F32)
            for g in range(2):
                for u in range(2):
                    nc.tensor.transpose(bank[:, u, g, :], words[:, 256 * g + u:256 * (g + 1):2], ident[:])

        def empty_turn(s, i):
            if i == 0:
                xg[s] = work.tile([P, 2, 2, P * 4], BF16, name="xg", align_bytes=64)
            nc.vector.tensor_tensor(
                out=xg[s][:, i].rearrange("p g (r u e) -> p g r u e", u=2, e=2),
                in0=xt[s, i][:].bitcast(BF16).rearrange("p u g (r e) -> p g r u e", e=2),
                in1=scale_cols[:].rearrange("p g (u e) -> p g u e", u=2).unsqueeze(2).to_broadcast([P, 2, P, 2, 2]),
                op=ALU.mult,
            )

        def quant_x(s):
            codes = work.tile([P, 2, 2, P], U32, name="xcodes", align_bytes=64)
            scales = work.tile([P, 2, 2, P], U8, name="xscales", align_bytes=64)
            xc[s] = (codes, scales)
            nc.vector.quantize_mx(
                out=codes[:].rearrange("p i g r -> p (i g r)").bitcast(FP8X4),
                scales=scales[:].rearrange("p i g r -> p (i g r)"),
                in_=xg[s][:].rearrange("p i g c -> p (i g c)"),
            )

        def down(s, i):
            bank = psum.tile([P, 4, P], F32, name="lat")
            lat[s, i] = bank
            codes, scales = xc[s]
            for t in range(4):
                for g in range(2):
                    nc.tensor.matmul_mx(
                        out=bank[:, t, :],
                        lhsT=wd_codes[:, g, t * P:(t + 1) * P].bitcast(FP8X4),
                        lhsT_scale=wd_scales[:, g, t * P:(t + 1) * P],
                        rhs=codes[:, i, g].bitcast(FP8X4),
                        rhs_scale=scales[:, i, g],
                        start=(g == 0),
                        stop=(g == 1),
                    )

        def empty_down(s, i):
            if i == 0:
                lg[s] = work.tile([P, 2, P, 4], BF16, name="lg", align_bytes=64, bufs=4)
            nc.scalar.copy(out=lg[s][:, i], in_=lat[s, i][:].rearrange("p t r -> p r t"))

        def quant_lat(s):
            codes = work.tile([P, 2, P], U32, name="lcodes", align_bytes=64)
            scales = work.tile([P, 2, P], U8, name="lscales", align_bytes=64)
            lc[s] = (codes, scales)
            nc.vector.quantize_mx(
                out=codes[:].rearrange("p i r -> p (i r)").bitcast(FP8X4),
                scales=scales[:].rearrange("p i r -> p (i r)"),
                in_=lg[s][:].rearrange("p i r t -> p (i r t)"),
            )

        def expand(s, i):
            if s % 2 == 0 and i == 0:
                rope[s // 2] = psum.tile([P, GROUP, H, 2, HALF], F32, name="rope")
            bank = psum.tile([P, 4, DH], F32, name="main")
            main[s, i] = bank
            codes, scales = lc[s]
            nc.tensor.matmul_mx(
                out=bank[:].rearrange("p a f -> p (a f)"),
                lhsT=codes[:, i].bitcast(FP8X4), lhsT_scale=scales[:, i],
                rhs=wu_main_codes[:].bitcast(FP8X4), rhs_scale=wu_main_scales[:],
                start=True, stop=True,
            )
            nc.tensor.matmul_mx(
                out=rope[s // 2][:, 2 * (s % 2) + i].rearrange("p h a f -> p (h a f)"),
                lhsT=codes[:, i].bitcast(FP8X4), lhsT_scale=scales[:, i],
                rhs=wu_rope_codes[:].bitcast(FP8X4), rhs_scale=wu_rope_scales[:],
                start=True, stop=True,
            )

        def empty_main(s, i):
            if s % 2 == 0 and i == 0:
                kv[s // 2] = outp.tile([P, GROUP, 4, DH + DR], F32, name="kv")
            nc.scalar.copy(out=kv[s // 2][:, 2 * (s % 2) + i, :, 0:DH], in_=main[s, i][:])

        rot = {}

        def rope_mul(g, lo, n):
            a = work.tile([P, n, H, 2, HALF], F32, name="rot_a", bufs=3)
            b = work.tile([P, n, H, 2, HALF], F32, name="rot_b", bufs=3)
            rot[g, lo] = (a, b)
            first = (g % POS_GROUPS) * GROUP + lo
            bank = rope[g][:, lo:lo + n]
            nc.vector.tensor_tensor(
                out=a[:].rearrange("p i h a f -> p i (h a) f"),
                in0=bank.rearrange("p i h a f -> p i (h a) f"),
                in1=cos[:, first:first + n].unsqueeze(2).to_broadcast([P, n, 2 * H, HALF]),
                op=ALU.mult,
            )
            nc.vector.tensor_tensor(
                out=b[:].rearrange("p i h a f -> p i h (a f)"),
                in0=bank.rearrange("p i h a f -> p i h (a f)"),
                in1=sin[:, first:first + n].rearrange("p i a f -> p i (a f)").unsqueeze(2).to_broadcast([P, n, H, DR]),
                op=ALU.mult,
            )

        def rope_add(g, lo, n):
            a, b = rot[g, lo]
            nc.vector.tensor_tensor(
                out=kv[g][:, lo:lo + n, 0:H, DH:].rearrange("p i h (a f) -> p i h a f", a=2),
                in0=a[:], in1=b[:, :, :, ::-1, :], op=ALU.add,
            )

        def rope_add_beside(g):
            a, b = rot[g, 0]
            for half in range(2):
                nc.gpsimd.tensor_tensor(
                    out=kv[g][:, :, 0:H, DH + half * HALF:DH + (half + 1) * HALF],
                    in0=a[:, :, :, half], in1=b[:, :, :, 1 - half], op=ALU.add,
                )

        def store_v(g):
            for h in range(H):
                nc.sync.dma_start(out=v_view[g][:, :, h], in_=kv[g][:, :, 2 + h, 0:DH])

        def store_k(g, lo, n):
            nc.sync.dma_start(out=k_view[g][:, lo:lo + n], in_=kv[g][:, lo:lo + n, 0:2, :].rearrange("p i h f -> p i (h f)"))

        for it in range(-2, STEPS + 4):
            wide, now, mid, lat_q, old, mul = it + 2, it, it - 1, it - 3, it - 4, it - 5
            if it == 1:
                quant_down(1)
            if 0 <= now < STEPS:
                turn(now, 0)
            if 0 <= lat_q < STEPS:
                quant_lat(lat_q)
            if 0 <= old < STEPS:
                expand(old, 0)
                expand(old, 1)
            if 0 <= now < STEPS:
                turn(now, 1)
            if 0 <= mid < STEPS:
                quant_x(mid)
                down(mid, 0)
                down(mid, 1)
            if 0 <= mul < STEPS - 1 and mul % 2:
                rope_mul(mul // 2, 0, GROUP)
                rope_add_beside(mul // 2)
            if 0 <= now < STEPS:
                empty_turn(now, 0)
                empty_turn(now, 1)
            if it == 2:
                quant_up()
            if 0 <= old < STEPS:
                empty_main(old, 0)
                empty_main(old, 1)
                if old % 2:
                    store_v(old // 2)
            if wide < STEPS:
                widen(wide, 0)
            if 0 <= mid < STEPS:
                empty_down(mid, 0)
                empty_down(mid, 1)
            if wide < STEPS:
                widen(wide, 1)
            if it == -2:
                group_down(1, nc.scalar.copy)
            if it == 0:
                group_up()
            if it == 3:
                tables()
            if 0 <= mul < STEPS - 1 and mul % 2:
                store_k(mul // 2, 0, GROUP)
        last = N_GROUPS - 1
        rope_mul(last, 0, 2)
        rope_mul(last, 2, 2)
        for lo in (0, 2):
            rope_add(last, lo, 2)
            store_k(last, lo, 2)
